import numpy as np
import ml_dtypes


def mxq(x, axis, fmt="e4m3"):
    dtype, down = {"e4m3": (ml_dtypes.float8_e4m3fn, 7), "e5m2": (ml_dtypes.float8_e5m2, 14)}[fmt]
    v = np.moveaxis(np.asarray(x, np.float32).astype(ml_dtypes.bfloat16).astype(np.float64), axis, -1)
    blocks = v.reshape(v.shape[:-1] + (-1, 32))
    amax = np.abs(blocks).max(-1, keepdims=True)
    byte = np.maximum(np.where(amax > 0, np.frexp(amax)[1] - 1 + 127, 0) - down, 1)
    scale = np.exp2(byte - 127.0)
    codes = (blocks / scale).astype(np.float32).astype(dtype).astype(np.float64)
    return np.moveaxis((codes * scale).reshape(v.shape), -1, axis)


WIDE = False


def mx_kscale(k):
    if not WIDE:
        return np.ones(k)
    levels = np.array([10, -10, 5, -5, 0])
    if k % 512:
        return np.exp2(np.random.permutation(np.resize(levels, k // 32))).repeat(32)
    a = np.empty((k // 512, 16))
    for p in range(k // 512):
        a[p, :8] = np.random.permutation(np.resize(levels, 8))
        for g in range(8):
            far = levels[np.abs(levels - a[p, g]) >= 10]
            a[p, g + 8] = far[np.random.randint(len(far))]
    return np.exp2(a.ravel()).repeat(32)


BF16 = ml_dtypes.bfloat16


def bf(x):
    return np.asarray(x, np.float32).astype(BF16)


def f64(x):
    return np.asarray(x).astype(np.float64)


G, D1, D2, D3, K, N = 4, 8, 16, 16, 1024, 256

EPS = 1e-6


def setup_inputs():
    s = mx_kscale(K)
    rows = np.random.standard_normal((G, D1, D2, D3, K))
    rows = rows * (0.5 + 1.5 * np.random.random_sample((G, D1, D2, D3, 1))) + 0.5 * np.random.standard_normal((G, D1, D2, D3, 1))
    return {"x": bf(rows.reshape(G * K, D1, D2, D3)),
            "ln_gamma": bf((1.0 + 0.1 * np.random.standard_normal((G, K))) * s),
            "ln_beta": bf(0.1 * np.random.standard_normal((G, K)) * s),
            "W": bf(np.random.standard_normal((G, N, K)) / np.sqrt(K) / s),
            "b": bf(0.1 * np.random.standard_normal((G, N)))}


def reference(x, ln_gamma, ln_beta, W, b):
    xg = f64(x).reshape(G, D1, D2, D3, K)
    mu = np.mean(xg, axis=-1, keepdims=True)
    var = np.mean(np.square(xg - mu), axis=-1, keepdims=True)
    xn = (xg - mu) / np.sqrt(var + EPS)
    xn = xn * f64(ln_gamma)[:, None, None, None, :] + f64(ln_beta)[:, None, None, None, :]
    a = mxq(xn.reshape(G, D1 * D2 * D3, K), 2, "e4m3")
    y = a @ mxq(f64(W), 2, "e4m3").transpose(0, 2, 1)
    y = y.reshape(G, D1, D2, D3, N) + f64(b)[:, None, None, None, :]
    y = np.moveaxis(y, 0, -2).reshape(D1, D2, D3, G * N)
    return np.transpose(y, (3, 0, 1, 2))

@@ -1,0 +1,317 @@
+from contextlib import ExitStack
+
+import concourse.mybir as mybir
+from concourse.masks import make_identity
+
+F32 = mybir.dt.float32
+BF16 = mybir.dt.bfloat16
+U32 = mybir.dt.uint32
+U8 = mybir.dt.uint8
+FP8X4 = mybir.dt.float8_e4m3fn_x4
+ALU = mybir.AluOpType
+ACT = mybir.ActivationFunctionType
+
+P = 128
+G = 4
+K = 1024
+O = 256
+POS = 2048
+UNIT = 512
+UPG = POS // UNIT
+UNITS = G * UPG
+ROWT = UNIT // P
+CHUNKS = K // P
+PASSES = K // 512
+OT = O // P
+EPS = 1e-6
+XBUFS = 5
+
+FLOPS = 2 * G * POS * K * O
+
+Z_ENGINE = ("g", "g", "g", "s")
+Z_LAST = ("v", "v", "v", "v")
+S_COLS = 64
+
+
+def tile_groupedlinear_t_kernel(tc, x, ln_gamma, ln_beta, W, b, out):
+    nc = tc.nc
+    xv = x.rearrange("a (h b) c d -> (a h) (b c d)", h=2)
+    ov = out.rearrange("o a b c -> o (a b c)")
+
+    with ExitStack() as ctx:
+        const = ctx.enter_context(tc.tile_pool(name="const", bufs=1))
+        xpool = ctx.enter_context(tc.tile_pool(name="xpool", bufs=XBUFS))
+        zpool = ctx.enter_context(tc.tile_pool(name="zpool", bufs=12))
+        small = ctx.enter_context(tc.tile_pool(name="small", bufs=4))
+        plpool = ctx.enter_context(tc.tile_pool(name="plpool", bufs=3))
+        gqpool = ctx.enter_context(tc.tile_pool(name="gqpool", bufs=2))
+        xcpool = ctx.enter_context(tc.tile_pool(name="xcpool", bufs=3))
+        ypool = ctx.enter_context(tc.tile_pool(name="ypool", bufs=3))
+        wstage = ctx.enter_context(tc.tile_pool(name="wstage", bufs=2))
+        pst = ctx.enter_context(tc.psum_pool(name="pst", bufs=6))
+        psy = ctx.enter_context(tc.psum_pool(name="psy", bufs=2))
+        ctx.enter_context(tc.manual_schedule())
+
+        x_t = {}
+        mv_t = {}
+        std_t = {}
+        rstd_t = {}
+        negmu_t = {}
+        nmr_t = {}
+        z_t = {}
+        pl_t = {}
+        xc_t = {}
+        xsc_t = {}
+        wg_t = {}
+
+        def live(u):
+            return 0 <= u < UNITS
+
+        def load_x(u):
+            xt = xpool.tile([P, ROWT, K], BF16, tag="x", name="xt%d" % u)
+            rows = xv[u * UNIT:(u + 1) * UNIT, :].rearrange("(j p) k -> p j k", p=P)
+            if u == 0:
+                for j in range(ROWT):
+                    nc.sync.dma_start(out=xt[:, j, :], in_=rows[:, j, :])
+            else:
+                nc.sync.dma_start(out=xt[:], in_=rows)
+            x_t[u] = xt
+
+        w_raw = []
+        for g in range(G):
+            wr = const.tile([P, OT, K], BF16, name="wraw%d" % g)
+            w_raw.append(wr)
+
+        def load_w(g):
+            nc.sync.dma_start(out=w_raw[g][:], in_=W[g].rearrange("(t o) k -> o t k", t=OT))
+
+        load_x(0)
+        praw = const.tile([16, 512], BF16, name="praw")
+        prm = const.tile([P, 5, P], BF16, name="prm")
+        nc.vector.memset(prm[:], 0.0)
+        eps_t = const.tile([P, 1], F32, name="eps_t")
+        nc.vector.memset(eps_t[:], EPS)
+        nc.sync.dma_start(out=praw[0:8, :], in_=ln_gamma.rearrange("g (c p) -> (g c) p", p=512))
+        nc.sync.dma_start(out=praw[8:16, :], in_=ln_beta.rearrange("g (c p) -> (g c) p", p=512))
+        nc.sync.dma_start(out=prm[0:8, 4, :], in_=b.rearrange("g (c p) -> (g c) p", p=P))
+        load_w(0)
+        for u in range(1, XBUFS - 2):
+            load_x(u)
+
+        warm = const.tile([P, 1], F32, name="warm")
+        nc.scalar.activation(out=warm[:], in_=eps_t[:], func=ACT.Sqrt)
+
+        nc.scalar.copy(out=prm[0:16, 0:4, :].rearrange("p t (b i) -> p t b i", i=8),
+                       in_=praw[:].rearrange("p (b t i) -> p t b i", t=4, i=8))
+
+        ident_b = const.tile([P, P], BF16, name="ident_b")
+        make_identity(nc, ident_b[:])
+        ident_f = const.tile([P, P], F32, name="ident_f")
+        make_identity(nc, ident_f[:])
+
+        prm_ps = pst.tile([P, 5, P], BF16, tag="zt", name="prm_ps")
+        for t in range(5):
+            nc.tensor.transpose(prm_ps[:, t, :], prm[:, t, :], ident_b[:])
+        cols = const.tile([P, 5, 16], F32, name="cols")
+        nc.scalar.copy(out=cols[:], in_=prm_ps[:, :, 0:16])
+
+        wc = const.tile([P, G, PASSES, O], U32, name="wc", align_bytes=64)
+        ws = const.tile([P, G, PASSES, O], U8, name="ws", align_bytes=64)
+
+        wp_t = {}
+
+        def w_permute(g):
+            wp = wstage.tile([P, OT, 4, K // 4], BF16, tag="wp", name="wp%d" % g)
+            for a in range(OT):
+                nc.scalar.copy(out=wp[:, a, :, :].rearrange("p t (b i) -> p t b i", i=8),
+                               in_=w_raw[g][:, a, :].rearrange("p (b t i) -> p t b i", t=4, i=8))
+            wp_t[g] = wp
+
+        def w_transpose(g, c2):
+            wt = pst.tile([P, OT, 4, P], BF16, tag="zt", name="wt%d_%d" % (g, c2))
+            for a in range(OT):
+                for t in range(4):
+                    nc.tensor.transpose(wt[:, a, t, :], wp_t[g][:, a, t, c2 * P:(c2 + 1) * P], ident_b[:])
+            wg = wstage.tile([P, OT, P, 4], BF16, tag="wg", name="wg%d_%d" % (g, c2), align_bytes=64)
+            nc.scalar.copy(out=wg[:], in_=wt[:].rearrange("p a t o -> p a o t"))
+            wg_t[(g, c2)] = wg
+
+        def w_quantise(g, c2):
+            nc.vector.quantize_mx(
+                out=wc[:, g, c2, :].bitcast(FP8X4),
+                scales=ws[:, g, c2, :],
+                in_=wg_t[(g, c2)][:].rearrange("p a o t -> p (a o t)"),
+            )
+
+        w_when = {}
+        for g in range(G):
+            w_when[max(UPG * g - 2, -1)] = (g, 0)
+            w_when[max(UPG * g - 1, 0)] = (g, 1)
+
+        w_perm = {max(UPG * g - 3, -1): g for g in range(G)}
+
+        st_t = {}
+
+        def bn(u, j, h):
+            if u not in st_t:
+                st_t[u] = small.tile([P, ROWT, 2, 6], F32, tag="st", name="st%d" % u)
+                mv_t[u] = small.tile([P, ROWT, 2], F32, tag="mv", name="mv%d" % u)
+            nc.vector.bn_stats(out=st_t[u][:, j, h, :], in_=x_t[u][:, j, h * 512:(h + 1) * 512])
+
+        def aggr(u, j):
+            nc.vector.bn_aggr(out=mv_t[u][:, j, :], in_=st_t[u][:, j, :, :].rearrange("p h s -> p (h s)"))
+
+        def sqrt_(u):
+            std = small.tile([P, ROWT], F32, tag="std", name="std%d" % u)
+            nc.scalar.activation(out=std[:], in_=mv_t[u][:, :, 1], func=ACT.Sqrt, bias=eps_t[:], scale=1.0)
+            std_t[u] = std
+
+        def recip(u):
+            rstd_t[u] = small.tile([P, ROWT], F32, tag="rstd", name="rstd%d" % u)
+            nc.vector.reciprocal(out=rstd_t[u][:], in_=std_t[u][:])
+
+        def negmean(u):
+            negmu_t[u] = small.tile([P, ROWT], F32, tag="negmu", name="negmu%d" % u)
+            nc.scalar.activation(out=negmu_t[u][:], in_=mv_t[u][:, :, 0], func=ACT.Copy, scale=-1.0)
+
+        def negmean_rstd(u):
+            nmr_t[u] = small.tile([P, ROWT], F32, tag="nmr", name="nmr%d" % u)
+            for j in range(ROWT):
+                if Z_ENGINE[j] == "s":
+                    nc.scalar.activation(out=nmr_t[u][:, j:j + 1], in_=negmu_t[u][:, j:j + 1], func=ACT.Copy,
+                                         scale=rstd_t[u][:, j:j + 1])
+
+        def zrow(u, j, eng):
+            zt = zpool.tile([P, 4, K // 4], F32, tag="z", name="z%d_%d" % (u, j))
+            z = zt[:].rearrange("p t (b i) -> p t b i", i=8)
+            xin = x_t[u][:, j, :].rearrange("p (b t i) -> p t b i", t=4, i=8)
+            if eng == "g":
+                nc.gpsimd.tensor_scalar(out=z, in0=xin, scalar1=negmu_t[u][:, j:j + 1],
+                                        scalar2=rstd_t[u][:, j:j + 1], op0=ALU.add, op1=ALU.mult)
+            elif eng == "v":
+                nc.vector.tensor_scalar(out=z, in0=xin, scalar1=negmu_t[u][:, j:j + 1],
+                                        scalar2=rstd_t[u][:, j:j + 1], op0=ALU.add, op1=ALU.mult)
+            else:
+                nc.scalar.activation(out=z, in_=xin, func=ACT.Identity,
+                                     scale=rstd_t[u][:, j:j + 1], bias=nmr_t[u][:, j:j + 1])
+            z_t[(u, j)] = zt
+
+        def bank(u, c):
+            g = u // UPG
+            zp = pst.tile([P, UNIT], F32, tag="zt", name="zp%d_%d" % (u, c))
+            c2, t = divmod(c, 4)
+            for j in range(ROWT):
+                nc.tensor.transpose(zp[:, j * P:(j + 1) * P], z_t[(u, j)][:, t, c2 * P:(c2 + 1) * P], ident_f[:])
+            gi = g * PASSES + c2
+            nc.scalar.activation(out=pl_t[u][:, c, :], in_=zp[:], func=ACT.Identity,
+                                 scale=cols[:, t, gi:gi + 1], bias=cols[:, t, 8 + gi:9 + gi])
+
+        gq_t = {}
+
+        def regroup(u, c2, eng, n0, n1):
+            if u not in gq_t:
+                gq_t[u] = gqpool.tile([P, PASSES, UNIT, 4], BF16, tag="gq", name="gq%d" % u, align_bytes=64)
+            dst = gq_t[u][:, c2, n0:n1, :].rearrange("p (c i) t -> p c t i", i=4)
+            src = pl_t[u][:, c2 * 4:(c2 + 1) * 4, n0:n1].rearrange("p t (c i) -> p c t i", i=4)
+            if eng == "v":
+                nc.vector.tensor_copy(out=dst, in_=src)
+            else:
+                nc.scalar.copy(out=dst, in_=src)
+
+        def quantise(u, c2):
+            if u not in xc_t:
+                xc_t[u] = xcpool.tile([P, PASSES, UNIT], U32, tag="xc", name="xc%d" % u, align_bytes=64)
+                xsc_t[u] = xcpool.tile([P, PASSES, UNIT], U8, tag="xsc", name="xsc%d" % u, align_bytes=64)
+            nc.vector.quantize_mx(
+                out=xc_t[u][:, c2, :].bitcast(FP8X4),
+                scales=xsc_t[u][:, c2, :],
+                in_=gq_t[u][:, c2, :, :].rearrange("p n t -> p (n t)"),
+            )
+
+        def multiply_store(u):
+            g = u // UPG
+            q = u % UPG
+            last = u == UNITS - 1
+            ysb = ypool.tile([P, OT, UNIT], F32, tag="y", name="y%d" % u)
+            yps = []
+            for a in range(OT):
+                yp = psy.tile([P, UNIT], F32, tag="yp", name="yp%d_%d" % (u, a))
+                yps.append(yp)
+            for c2 in range(PASSES):
+                for a in range(OT):
+                    nc.tensor.matmul_mx(
+                        out=yps[a][:],
+                        lhsT=wc[:, g, c2, a * P:(a + 1) * P].bitcast(FP8X4),
+                        lhsT_scale=ws[:, g, c2, a * P:(a + 1) * P],
+                        rhs=xc_t[u][:, c2, :].bitcast(FP8X4),
+                        rhs_scale=xsc_t[u][:, c2, :],
+                        start=(c2 == 0),
+                        stop=(c2 == PASSES - 1),
+                    )
+            dst = ov[g * O:(g + 1) * O, q * UNIT:(q + 1) * UNIT].rearrange("(t o) n -> o t n", t=OT)
+            for a in range(OT):
+                bi = g * OT + a
+                if last and a == 1:
+                    nc.vector.tensor_scalar(out=ysb[:, a, :], in0=yps[a][:], scalar1=cols[:, 4, bi:bi + 1],
+                                            scalar2=None, op0=ALU.add)
+                else:
+                    nc.scalar.activation(out=ysb[:, a, :], in_=yps[a][:], func=ACT.Identity,
+                                         bias=cols[:, 4, bi:bi + 1], scale=1.0)
+                if last:
+                    nc.sync.dma_start(out=dst[:, a, :], in_=ysb[:, a, :])
+            if not last:
+                nc.sync.dma_start(out=dst, in_=ysb[:])
+
+        for i in range(-1, UNITS + 2):
+            if live(i + XBUFS - 1):
+                load_x(i + XBUFS - 1)
+            if i >= 0 and i % UPG == 0 and i // UPG + 1 < G:
+                load_w(i // UPG + 1)
+            if live(i):
+                sqrt_(i)
+                negmean(i)
+            last_a = i - 2 == UNITS - 1
+            if live(i - 2):
+                regroup(i - 2, 0, "v", 0, UNIT)
+                if not last_a:
+                    regroup(i - 2, 1, "v", 0, UNIT - S_COLS)
+                quantise(i - 2, 0)
+            if (i - 1) in w_when:
+                w_quantise(*w_when[i - 1])
+            if last_a:
+                regroup(i - 2, 1, "v", 0, UNIT)
+            if live(i):
+                recip(i)
+            if live(i - 2):
+                quantise(i - 2, 1)
+            z_eng = Z_LAST if i == UNITS - 1 else Z_ENGINE
+            if live(i):
+                for j in range(ROWT):
+                    if z_eng[j] != "s":
+                        zrow(i, j, z_eng[j])
+            if live(i - 1):
+                pl_t[i - 1] = plpool.tile([P, CHUNKS, UNIT], BF16, tag="pl", name="pl%d" % (i - 1))
+                for c in range(CHUNKS):
+                    bank(i - 1, c)
+                    if c == 5 and live(i) and "s" in z_eng:
+                        negmean_rstd(i)
+            elif live(i) and "s" in z_eng:
+                negmean_rstd(i)
+            if live(i):
+                for j in range(ROWT):
+                    if z_eng[j] == "s":
+                        zrow(i, j, "s")
+            if live(i - 1) and i - 1 != UNITS - 1:
+                regroup(i - 1, 1, "s", UNIT - S_COLS, UNIT)
+            if live(i - 2):
+                multiply_store(i - 2)
+            if i in w_perm:
+                w_permute(w_perm[i])
+            if i in w_when:
+                w_transpose(*w_when[i])
+            if live(i + 1):
+                for j in range(ROWT):
+                    bn(i + 1, j, 0)
+                    bn(i + 1, j, 1)
+                for j in range(ROWT):
+                    aggr(i + 1, j)

@@ -30,7 +30,7 @@ FLOPS = 2 * G * POS * K * O
 
 Z_ENGINE = ("g", "g", "g", "s")
 Z_LAST = ("v", "v", "v", "v")
-S_COLS = 64
+S_COLS = 128
 
 
 def tile_groupedlinear_t_kernel(tc, x, ln_gamma, ln_beta, W, b, out):
@@ -86,13 +86,13 @@ def tile_groupedlinear_t_kernel(tc, x, ln_gamma, ln_beta, W, b, out):
             nc.sync.dma_start(out=w_raw[g][:], in_=W[g].rearrange("(t o) k -> o t k", t=OT))
 
         load_x(0)
-        praw = const.tile([16, 512], BF16, name="praw")
         prm = const.tile([P, 5, P], BF16, name="prm")
         nc.vector.memset(prm[:], 0.0)
+        prmk = prm[:, 0:4, :].rearrange("p t q -> p (t q)")
         eps_t = const.tile([P, 1], F32, name="eps_t")
         nc.vector.memset(eps_t[:], EPS)
-        nc.sync.dma_start(out=praw[0:8, :], in_=ln_gamma.rearrange("g (c p) -> (g c) p", p=512))
-        nc.sync.dma_start(out=praw[8:16, :], in_=ln_beta.rearrange("g (c p) -> (g c) p", p=512))
+        nc.sync.dma_start(out=prmk[0:8, :], in_=ln_gamma.rearrange("g (c p) -> (g c) p", p=512))
+        nc.sync.dma_start(out=prmk[8:16, :], in_=ln_beta.rearrange("g (c p) -> (g c) p", p=512))
         nc.sync.dma_start(out=prm[0:8, 4, :], in_=b.rearrange("g (c p) -> (g c) p", p=P))
         load_w(0)
         for u in range(1, XBUFS - 2):
@@ -101,39 +101,30 @@ def tile_groupedlinear_t_kernel(tc, x, ln_gamma, ln_beta, W, b, out):
         warm = const.tile([P, 1], F32, name="warm")
         nc.scalar.activation(out=warm[:], in_=eps_t[:], func=ACT.Sqrt)
 
-        nc.scalar.copy(out=prm[0:16, 0:4, :].rearrange("p t (b i) -> p t b i", i=8),
-                       in_=praw[:].rearrange("p (b t i) -> p t b i", t=4, i=8))
-
         ident_b = const.tile([P, P], BF16, name="ident_b")
         make_identity(nc, ident_b[:])
         ident_f = const.tile([P, P], F32, name="ident_f")
         make_identity(nc, ident_f[:])
 
         prm_ps = pst.tile([P, 5, P], BF16, tag="zt", name="prm_ps")
-        for t in range(5):
-            nc.tensor.transpose(prm_ps[:, t, :], prm[:, t, :], ident_b[:])
+        for t in range(4):
+            nc.tensor.transpose(prm_ps[:, t, :], prmk[:, t:512:4], ident_b[:])
+        nc.tensor.transpose(prm_ps[:, 4, :], prm[:, 4, :], ident_b[:])
         cols = const.tile([P, 5, 16], F32, name="cols")
         nc.scalar.copy(out=cols[:], in_=prm_ps[:, :, 0:16])
 
         wc = const.tile([P, G, PASSES, O], U32, name="wc", align_bytes=64)
         ws = const.tile([P, G, PASSES, O], U8, name="ws", align_bytes=64)
 
-        wp_t = {}
-
-        def w_permute(g):
-            wp = wstage.tile([P, OT, 4, K // 4], BF16, tag="wp", name="wp%d" % g)
-            for a in range(OT):
-                nc.scalar.copy(out=wp[:, a, :, :].rearrange("p t (b i) -> p t b i", i=8),
-                               in_=w_raw[g][:, a, :].rearrange("p (b t i) -> p t b i", t=4, i=8))
-            wp_t[g] = wp
-
         def w_transpose(g, c2):
-            wt = pst.tile([P, OT, 4, P], BF16, tag="zt", name="wt%d_%d" % (g, c2))
+            wt = pst.tile([P, OT, 2, P], F32, tag="zt", name="wt%d_%d" % (g, c2))
             for a in range(OT):
-                for t in range(4):
-                    nc.tensor.transpose(wt[:, a, t, :], wp_t[g][:, a, t, c2 * P:(c2 + 1) * P], ident_b[:])
+                words = w_raw[g][:, a, :].bitcast(F32)
+                for e in range(2):
+                    nc.tensor.transpose(wt[:, a, e, :], words[:, c2 * 256 + e:(c2 + 1) * 256:2], ident_f[:])
             wg = wstage.tile([P, OT, P, 4], BF16, tag="wg", name="wg%d_%d" % (g, c2), align_bytes=64)
-            nc.scalar.copy(out=wg[:], in_=wt[:].rearrange("p a t o -> p a o t"))
+            nc.scalar.copy(out=wg[:].rearrange("p a o t -> p (a o t)").bitcast(F32).rearrange("p (a o e) -> p a o e", a=OT, e=2),
+                           in_=wt[:].rearrange("p a e o -> p a o e"))
             wg_t[(g, c2)] = wg
 
         def w_quantise(g, c2):
@@ -148,7 +139,6 @@ def tile_groupedlinear_t_kernel(tc, x, ln_gamma, ln_beta, W, b, out):
             w_when[max(UPG * g - 2, -1)] = (g, 0)
             w_when[max(UPG * g - 1, 0)] = (g, 1)
 
-        w_perm = {max(UPG * g - 3, -1): g for g in range(G)}
 
         st_t = {}
 
@@ -183,8 +173,8 @@ def tile_groupedlinear_t_kernel(tc, x, ln_gamma, ln_beta, W, b, out):
 
         def zrow(u, j, eng):
             zt = zpool.tile([P, 4, K // 4], F32, tag="z", name="z%d_%d" % (u, j))
-            z = zt[:].rearrange("p t (b i) -> p t b i", i=8)
-            xin = x_t[u][:, j, :].rearrange("p (b t i) -> p t b i", t=4, i=8)
+            z = zt[:]
+            xin = x_t[u][:, j, :].rearrange("p (q t) -> p t q", t=4)
             if eng == "g":
                 nc.gpsimd.tensor_scalar(out=z, in0=xin, scalar1=negmu_t[u][:, j:j + 1],
                                         scalar2=rstd_t[u][:, j:j + 1], op0=ALU.add, op1=ALU.mult)
@@ -305,8 +295,6 @@ def tile_groupedlinear_t_kernel(tc, x, ln_gamma, ln_beta, W, b, out):
                 regroup(i - 1, 1, "s", UNIT - S_COLS, UNIT)
             if live(i - 2):
                 multiply_store(i - 2)
-            if i in w_perm:
-                w_permute(w_perm[i])
             if i in w_when:
                 w_transpose(*w_when[i])
             if live(i + 1):

@@ -23,14 +23,26 @@ ROWT = UNIT // P
 CHUNKS = K // P
 PASSES = K // 512
 OT = O // P
+HALF = UNIT // 2
 EPS = 1e-6
-XBUFS = 5
+XBUFS = 6
 
 FLOPS = 2 * G * POS * K * O
 
 Z_ENGINE = ("g", "g", "g", "s")
 Z_LAST = ("v", "v", "v", "v")
-S_COLS = 128
+N_LAST = 1
+S_COLS = 160
+S_LAST = 128
+S_STATS = {0: (3,)}
+LATE = ()
+G_T = 0
+X0_ORDER = (0, 3, 1, 2)
+SPLIT = True
+DEFER = ()
+FIRST = 1
+FIRST1 = 3
+V_BANKS = {}
 
 
 def tile_groupedlinear_t_kernel(tc, x, ln_gamma, ln_beta, W, b, out):
@@ -47,6 +59,7 @@ def tile_groupedlinear_t_kernel(tc, x, ln_gamma, ln_beta, W, b, out):
         gqpool = ctx.enter_context(tc.tile_pool(name="gqpool", bufs=2))
         xcpool = ctx.enter_context(tc.tile_pool(name="xcpool", bufs=3))
         ypool = ctx.enter_context(tc.tile_pool(name="ypool", bufs=3))
+        junkpool = ctx.enter_context(tc.tile_pool(name="junkpool", bufs=1))
         wstage = ctx.enter_context(tc.tile_pool(name="wstage", bufs=2))
         pst = ctx.enter_context(tc.psum_pool(name="pst", bufs=6))
         psy = ctx.enter_context(tc.psum_pool(name="psy", bufs=2))
@@ -71,7 +84,7 @@ def tile_groupedlinear_t_kernel(tc, x, ln_gamma, ln_beta, W, b, out):
             xt = xpool.tile([P, ROWT, K], BF16, tag="x", name="xt%d" % u)
             rows = xv[u * UNIT:(u + 1) * UNIT, :].rearrange("(j p) k -> p j k", p=P)
             if u == 0:
-                for j in range(ROWT):
+                for j in X0_ORDER:
                     nc.sync.dma_start(out=xt[:, j, :], in_=rows[:, j, :])
             else:
                 nc.sync.dma_start(out=xt[:], in_=rows)
@@ -94,8 +107,9 @@ def tile_groupedlinear_t_kernel(tc, x, ln_gamma, ln_beta, W, b, out):
         nc.sync.dma_start(out=prmk[0:8, :], in_=ln_gamma.rearrange("g (c p) -> (g c) p", p=512))
         nc.sync.dma_start(out=prmk[8:16, :], in_=ln_beta.rearrange("g (c p) -> (g c) p", p=512))
         nc.sync.dma_start(out=prm[0:8, 4, :], in_=b.rearrange("g (c p) -> (g c) p", p=P))
+        load_x(1)
         load_w(0)
-        for u in range(1, XBUFS - 2):
+        for u in range(2, XBUFS - 1):
             load_x(u)
 
         warm = const.tile([P, 1], F32, name="warm")
@@ -106,12 +120,14 @@ def tile_groupedlinear_t_kernel(tc, x, ln_gamma, ln_beta, W, b, out):
         ident_f = const.tile([P, P], F32, name="ident_f")
         make_identity(nc, ident_f[:])
 
-        prm_ps = pst.tile([P, 5, P], BF16, tag="zt", name="prm_ps")
-        for t in range(4):
-            nc.tensor.transpose(prm_ps[:, t, :], prmk[:, t:512:4], ident_b[:])
-        nc.tensor.transpose(prm_ps[:, 4, :], prm[:, 4, :], ident_b[:])
         cols = const.tile([P, 5, 16], F32, name="cols")
-        nc.scalar.copy(out=cols[:], in_=prm_ps[:, :, 0:16])
+
+        def parameters():
+            prm_ps = pst.tile([P, 5, P], BF16, tag="zt", name="prm_ps")
+            for t in range(4):
+                nc.tensor.transpose(prm_ps[:, t, :], prmk[:, t:512:4], ident_b[:])
+            nc.tensor.transpose(prm_ps[:, 4, :], prm[:, 4, :], ident_b[:])
+            nc.scalar.copy(out=cols[:], in_=prm_ps[:, :, 0:16])
 
         wc = const.tile([P, G, PASSES, O], U32, name="wc", align_bytes=64)
         ws = const.tile([P, G, PASSES, O], U8, name="ws", align_bytes=64)
@@ -135,46 +151,63 @@ def tile_groupedlinear_t_kernel(tc, x, ln_gamma, ln_beta, W, b, out):
             )
 
         w_when = {}
-        for g in range(G):
-            w_when[max(UPG * g - 2, -1)] = (g, 0)
-            w_when[max(UPG * g - 1, 0)] = (g, 1)
+        for g in range(1, G):
+            w_when[UPG * g - 2] = (g, 0)
+            w_when[UPG * g - 1] = (g, 1)
 
 
         st_t = {}
 
-        def bn(u, j, h):
+        def stat_tiles(u):
             if u not in st_t:
                 st_t[u] = small.tile([P, ROWT, 2, 6], F32, tag="st", name="st%d" % u)
                 mv_t[u] = small.tile([P, ROWT, 2], F32, tag="mv", name="mv%d" % u)
+                std_t[u] = small.tile([P, ROWT], F32, tag="std", name="std%d" % u)
+                negmu_t[u] = small.tile([P, ROWT], F32, tag="negmu", name="negmu%d" % u)
+                rstd_t[u] = small.tile([P, ROWT], F32, tag="rstd", name="rstd%d" % u)
+                nmr_t[u] = small.tile([P, ROWT], F32, tag="nmr", name="nmr%d" % u)
+
+        def v_rows(u):
+            return [j for j in range(ROWT) if j not in S_STATS.get(u, ())]
+
+        def bn(u, j, h):
+            stat_tiles(u)
             nc.vector.bn_stats(out=st_t[u][:, j, h, :], in_=x_t[u][:, j, h * 512:(h + 1) * 512])
 
         def aggr(u, j):
             nc.vector.bn_aggr(out=mv_t[u][:, j, :], in_=st_t[u][:, j, :, :].rearrange("p h s -> p (h s)"))
 
-        def sqrt_(u):
-            std = small.tile([P, ROWT], F32, tag="std", name="std%d" % u)
-            nc.scalar.activation(out=std[:], in_=mv_t[u][:, :, 1], func=ACT.Sqrt, bias=eps_t[:], scale=1.0)
-            std_t[u] = std
+        acc_t = {}
 
-        def recip(u):
-            rstd_t[u] = small.tile([P, ROWT], F32, tag="rstd", name="rstd%d" % u)
-            nc.vector.reciprocal(out=rstd_t[u][:], in_=std_t[u][:])
+        def scalar_sum(u, j):
+            stat_tiles(u)
+            junk = junkpool.tile([P, K], BF16, tag="junk", name="junka%d_%d" % (u, j))
+            acc_t[(u, j)] = small.tile([P, 2], F32, tag="acc", name="acc%d_%d" % (u, j))
+            nc.scalar.activation(out=junk[:], in_=x_t[u][:, j, :], func=ACT.Identity, accum_out=acc_t[(u, j)][:, 0:1])
+            nc.scalar.activation(out=negmu_t[u][:, j:j + 1], in_=acc_t[(u, j)][:, 0:1], func=ACT.Copy, scale=-1.0 / K)
 
-        def negmean(u):
-            negmu_t[u] = small.tile([P, ROWT], F32, tag="negmu", name="negmu%d" % u)
-            nc.scalar.activation(out=negmu_t[u][:], in_=mv_t[u][:, :, 0], func=ACT.Copy, scale=-1.0)
+        def scalar_square(u, j):
+            junk = junkpool.tile([P, K], BF16, tag="junk", name="junkb%d_%d" % (u, j))
+            nc.scalar.activation(out=junk[:], in_=x_t[u][:, j, :], func=ACT.Square, scale=1.0,
+                                 bias=negmu_t[u][:, j:j + 1], accum_out=acc_t[(u, j)][:, 1:2])
+            nc.scalar.activation(out=std_t[u][:, j:j + 1], in_=acc_t[(u, j)][:, 1:2], func=ACT.Sqrt, bias=eps_t[:], scale=1.0 / K)
 
-        def negmean_rstd(u):
-            nmr_t[u] = small.tile([P, ROWT], F32, tag="nmr", name="nmr%d" % u)
-            for j in range(ROWT):
-                if Z_ENGINE[j] == "s":
-                    nc.scalar.activation(out=nmr_t[u][:, j:j + 1], in_=negmu_t[u][:, j:j + 1], func=ACT.Copy,
-                                         scale=rstd_t[u][:, j:j + 1])
+        def sqrt_negmean(u, j0, j1):
+            nc.scalar.activation(out=std_t[u][:, j0:j1], in_=mv_t[u][:, j0:j1, 1], func=ACT.Sqrt, bias=eps_t[:], scale=1.0)
+            nc.scalar.activation(out=negmu_t[u][:, j0:j1], in_=mv_t[u][:, j0:j1, 0], func=ACT.Copy, scale=-1.0)
 
-        def zrow(u, j, eng):
-            zt = zpool.tile([P, 4, K // 4], F32, tag="z", name="z%d_%d" % (u, j))
-            z = zt[:]
-            xin = x_t[u][:, j, :].rearrange("p (q t) -> p t q", t=4)
+        def recip(u, j0=0, j1=ROWT):
+            nc.vector.reciprocal(out=rstd_t[u][:, j0:j1], in_=std_t[u][:, j0:j1])
+
+        def negmean_rstd(u, j):
+            nc.scalar.activation(out=nmr_t[u][:, j:j + 1], in_=negmu_t[u][:, j:j + 1], func=ACT.Copy,
+                                 scale=rstd_t[u][:, j:j + 1])
+
+        def zrow(u, j, eng, t0=0, t1=4):
+            if (u, j) not in z_t:
+                z_t[(u, j)] = zpool.tile([P, 4, K // 4], F32, tag="z", name="z%d_%d" % (u, j))
+            z = z_t[(u, j)][:, t0:t1, :]
+            xin = x_t[u][:, j, :].rearrange("p (q t) -> p t q", t=4)[:, t0:t1, :]
             if eng == "g":
                 nc.gpsimd.tensor_scalar(out=z, in0=xin, scalar1=negmu_t[u][:, j:j + 1],
                                         scalar2=rstd_t[u][:, j:j + 1], op0=ALU.add, op1=ALU.mult)
@@ -184,7 +217,6 @@ def tile_groupedlinear_t_kernel(tc, x, ln_gamma, ln_beta, W, b, out):
             else:
                 nc.scalar.activation(out=z, in_=xin, func=ACT.Identity,
                                      scale=rstd_t[u][:, j:j + 1], bias=nmr_t[u][:, j:j + 1])
-            z_t[(u, j)] = zt
 
         def bank(u, c):
             g = u // UPG
@@ -193,8 +225,12 @@ def tile_groupedlinear_t_kernel(tc, x, ln_gamma, ln_beta, W, b, out):
             for j in range(ROWT):
                 nc.tensor.transpose(zp[:, j * P:(j + 1) * P], z_t[(u, j)][:, t, c2 * P:(c2 + 1) * P], ident_f[:])
             gi = g * PASSES + c2
-            nc.scalar.activation(out=pl_t[u][:, c, :], in_=zp[:], func=ACT.Identity,
-                                 scale=cols[:, t, gi:gi + 1], bias=cols[:, t, 8 + gi:9 + gi])
+            if c in V_BANKS.get(u, ()):
+                nc.vector.tensor_scalar(out=pl_t[u][:, c, :], in0=zp[:], scalar1=cols[:, t, gi:gi + 1],
+                                        scalar2=cols[:, t, 8 + gi:9 + gi], op0=ALU.mult, op1=ALU.add)
+            else:
+                nc.scalar.activation(out=pl_t[u][:, c, :], in_=zp[:], func=ACT.Identity,
+                                     scale=cols[:, t, gi:gi + 1], bias=cols[:, t, 8 + gi:9 + gi])
 
         gq_t = {}
 
@@ -208,21 +244,20 @@ def tile_groupedlinear_t_kernel(tc, x, ln_gamma, ln_beta, W, b, out):
             else:
                 nc.scalar.copy(out=dst, in_=src)
 
-        def quantise(u, c2):
+        def quantise(u, c2, n0=0, n1=UNIT):
             if u not in xc_t:
                 xc_t[u] = xcpool.tile([P, PASSES, UNIT], U32, tag="xc", name="xc%d" % u, align_bytes=64)
                 xsc_t[u] = xcpool.tile([P, PASSES, UNIT], U8, tag="xsc", name="xsc%d" % u, align_bytes=64)
             nc.vector.quantize_mx(
-                out=xc_t[u][:, c2, :].bitcast(FP8X4),
-                scales=xsc_t[u][:, c2, :],
-                in_=gq_t[u][:, c2, :, :].rearrange("p n t -> p (n t)"),
+                out=xc_t[u][:, c2, n0:n1].bitcast(FP8X4),
+                scales=xsc_t[u][:, c2, n0:n1],
+                in_=gq_t[u][:, c2, n0:n1, :].rearrange("p n t -> p (n t)"),
             )
 
-        def multiply_store(u):
+        yps_t = {}
+
+        def multiply(u):
             g = u // UPG
-            q = u % UPG
-            last = u == UNITS - 1
-            ysb = ypool.tile([P, OT, UNIT], F32, tag="y", name="y%d" % u)
             yps = []
             for a in range(OT):
                 yp = psy.tile([P, UNIT], F32, tag="yp", name="yp%d_%d" % (u, a))
@@ -238,68 +273,172 @@ def tile_groupedlinear_t_kernel(tc, x, ln_gamma, ln_beta, W, b, out):
                         start=(c2 == 0),
                         stop=(c2 == PASSES - 1),
                     )
+            yps_t[u] = yps
+
+        last_t = {}
+
+        def last_product(h, c2):
+            u = UNITS - 1
+            g = G - 1
+            for a in range(OT):
+                if c2 == 0:
+                    last_t[(a, h)] = pst.tile([P, HALF], F32, tag="zt", name="ylast%d_%d" % (a, h))
+                nc.tensor.matmul_mx(
+                    out=last_t[(a, h)][:],
+                    lhsT=wc[:, g, c2, a * P:(a + 1) * P].bitcast(FP8X4),
+                    lhsT_scale=ws[:, g, c2, a * P:(a + 1) * P],
+                    rhs=xc_t[u][:, c2, h * HALF:(h + 1) * HALF].bitcast(FP8X4),
+                    rhs_scale=xsc_t[u][:, c2, h * HALF:(h + 1) * HALF],
+                    start=(c2 == 0),
+                    stop=(c2 == PASSES - 1),
+                )
+
+        def last_store(h, engines):
+            g = G - 1
+            if h == 0:
+                last_t["y"] = ypool.tile([P, OT, UNIT], F32, tag="y", name="ylast")
+            for a in range(OT):
+                bi = g * OT + a
+                src = last_t[(a, h)][:]
+                dst = last_t["y"][:, a, h * HALF:(h + 1) * HALF]
+                if engines[a] == "v":
+                    nc.vector.tensor_scalar(out=dst, in0=src, scalar1=cols[:, 4, bi:bi + 1], scalar2=None, op0=ALU.add)
+                else:
+                    nc.scalar.activation(out=dst, in_=src, func=ACT.Identity, bias=cols[:, 4, bi:bi + 1], scale=1.0)
+                p0 = (UPG - 1) * UNIT + h * HALF
+                nc.sync.dma_start(out=ov[bi * P:(bi + 1) * P, p0:p0 + HALF], in_=dst)
+
+        def store(u):
+            g = u // UPG
+            q = u % UPG
+            yps = yps_t[u]
+            ysb = ypool.tile([P, OT, UNIT], F32, tag="y", name="y%d" % u)
             dst = ov[g * O:(g + 1) * O, q * UNIT:(q + 1) * UNIT].rearrange("(t o) n -> o t n", t=OT)
             for a in range(OT):
                 bi = g * OT + a
-                if last and a == 1:
-                    nc.vector.tensor_scalar(out=ysb[:, a, :], in0=yps[a][:], scalar1=cols[:, 4, bi:bi + 1],
-                                            scalar2=None, op0=ALU.add)
-                else:
-                    nc.scalar.activation(out=ysb[:, a, :], in_=yps[a][:], func=ACT.Identity,
-                                         bias=cols[:, 4, bi:bi + 1], scale=1.0)
-                if last:
-                    nc.sync.dma_start(out=dst[:, a, :], in_=ysb[:, a, :])
-            if not last:
-                nc.sync.dma_start(out=dst, in_=ysb[:])
+                nc.scalar.activation(out=ysb[:, a, :], in_=yps[a][:], func=ACT.Identity,
+                                     bias=cols[:, 4, bi:bi + 1], scale=1.0)
+            nc.sync.dma_start(out=dst, in_=ysb[:])
 
-        for i in range(-1, UNITS + 2):
+        def z_engine(u):
+            return Z_LAST if u >= UNITS - N_LAST else Z_ENGINE
+
+        def s_cols(u):
+            return S_LAST if u == UNITS - 1 else S_COLS
+
+        def zrows(u, engines):
+            for j in range(ROWT):
+                if z_engine(u)[j] in engines:
+                    if z_engine(u)[j] == "s":
+                        negmean_rstd(u, j)
+                    zrow(u, j, z_engine(u)[j], G_T if z_engine(u)[j] == "s" else 0, 4)
+            if "g" in engines and z_engine(u)[3] == "s" and G_T:
+                zrow(u, 3, "g", 0, G_T)
+
+        s0 = S_STATS.get(0, ())
+        s1 = S_STATS.get(1, ())
+        n0 = ROWT - len(s0)
+        if s0:
+            scalar_sum(0, 3)
+        for j in range(n0):
+            bn(0, j, 0)
+            bn(0, j, 1)
+            if j:
+                recip(0, j - 1, j)
+                zrow(0, j - 1, "g")
+            aggr(0, j)
+            sqrt_negmean(0, j, j + 1)
+            if j == 0 and s0:
+                scalar_square(0, 3)
+        bn(1, 0, 0)
+        recip(0, n0 - 1, 4)
+        if s0:
+            zrow(0, 2, "g")
+        if s1:
+            scalar_sum(1, 3)
+        negmean_rstd(0, 3)
+        zrow(0, 3, "s")
+        bn(1, 0, 1)
+        if s1:
+            scalar_square(1, 3)
+        for j in range(1, ROWT):
+            if j not in s1:
+                bn(1, j, 0)
+                bn(1, j, 1)
+        for j in range(ROWT):
+            if j not in s1:
+                aggr(1, j)
+        parameters()
+
+        for i in range(UNITS + 1):
             if live(i + XBUFS - 1):
                 load_x(i + XBUFS - 1)
-            if i >= 0 and i % UPG == 0 and i // UPG + 1 < G:
+            if i % UPG == 0 and i // UPG + 1 < G:
                 load_w(i // UPG + 1)
-            if live(i):
-                sqrt_(i)
-                negmean(i)
-            last_a = i - 2 == UNITS - 1
-            if live(i - 2):
-                regroup(i - 2, 0, "v", 0, UNIT)
-                if not last_a:
-                    regroup(i - 2, 1, "v", 0, UNIT - S_COLS)
-                quantise(i - 2, 0)
-            if (i - 1) in w_when:
-                w_quantise(*w_when[i - 1])
-            if last_a:
-                regroup(i - 2, 1, "v", 0, UNIT)
-            if live(i):
-                recip(i)
-            if live(i - 2):
-                quantise(i - 2, 1)
-            z_eng = Z_LAST if i == UNITS - 1 else Z_ENGINE
-            if live(i):
-                for j in range(ROWT):
-                    if z_eng[j] != "s":
-                        zrow(i, j, z_eng[j])
+            if live(i - 2) and i not in LATE:
+                store(i - 2)
             if live(i - 1):
-                pl_t[i - 1] = plpool.tile([P, CHUNKS, UNIT], BF16, tag="pl", name="pl%d" % (i - 1))
-                for c in range(CHUNKS):
-                    bank(i - 1, c)
-                    if c == 5 and live(i) and "s" in z_eng:
-                        negmean_rstd(i)
-            elif live(i) and "s" in z_eng:
-                negmean_rstd(i)
+                regroup(i - 1, 0, "v", 0, UNIT)
+                if i - 1 < UNITS - 1:
+                    regroup(i - 1, 1, "v", 0, UNIT - s_cols(i - 1))
+                quantise(i - 1, 0)
+                if i - 1 in w_when:
+                    w_quantise(*w_when[i - 1])
+                if i == 1:
+                    w_quantise(0, 0)
+                    w_quantise(0, 1)
+                if i - 1 == UNITS - 1:
+                    last_product(0, 0)
+                    last_product(1, 0)
+                    regroup(i - 1, 1, "v", 0, HALF)
+                    regroup(i - 1, 1, "v", HALF, UNIT - s_cols(i - 1))
+                    quantise(i - 1, 1, 0, HALF)
+                    last_product(0, 1)
+                    quantise(i - 1, 1, HALF, UNIT)
+                    last_product(1, 1)
+                    last_store(0, "ss")
+                    last_store(1, "sv")
+            if i == 0:
+                bn(i + 2, 0, 0)
+                bn(i + 2, 0, 1)
+
+            def banks(c0, c1):
+                for c in range(c0, c1):
+                    bank(i, c)
+
+            first = FIRST if i else FIRST1
             if live(i):
-                for j in range(ROWT):
-                    if z_eng[j] == "s":
-                        zrow(i, j, "s")
-            if live(i - 1) and i - 1 != UNITS - 1:
-                regroup(i - 1, 1, "s", UNIT - S_COLS, UNIT)
-            if live(i - 2):
-                multiply_store(i - 2)
+                pl_t[i] = plpool.tile([P, CHUNKS, UNIT], BF16, tag="pl", name="pl%d" % i)
+                banks(0, first)
+            if live(i + 1):
+                sqrt_negmean(i + 1, 0, ROWT - len(S_STATS.get(i + 1, ())))
+                recip(i + 1)
+            if i in DEFER:
+                multiply(i - 2)
+                store(i - 2)
+            if live(i - 1) and i - 1 < UNITS - 1:
+                quantise(i - 1, 1)
+            if live(i + 1):
+                zrows(i + 1, "gv")
+            if live(i):
+                banks(first, CHUNKS)
+            if i in LATE and i not in DEFER:
+                store(i - 2)
+            if i == 0:
+                w_transpose(0, 0)
+                w_transpose(0, 1)
+            if live(i + 1):
+                zrows(i + 1, "s")
+            if live(i):
+                regroup(i, 1, "s", UNIT - s_cols(i), UNIT)
             if i in w_when:
                 w_transpose(*w_when[i])
-            if live(i + 1):
+            if live(i - 1) and i + 1 not in DEFER and i - 1 < UNITS - 1:
+                multiply(i - 1)
+            if live(i + 2):
                 for j in range(ROWT):
-                    bn(i + 1, j, 0)
-                    bn(i + 1, j, 1)
+                    for h in range(2):
+                        if i or j:
+                            bn(i + 2, j, h)
                 for j in range(ROWT):
-                    aggr(i + 1, j)
+                    aggr(i + 2, j)

@@ -32,10 +32,15 @@ FLOPS = 2 * G * POS * K * O
 Z_ENGINE = ("g", "g", "g", "s")
 Z_LAST = ("v", "v", "v", "v")
 N_LAST = 1
-S_COLS = 160
-S_LAST = 128
+S_COLS = 0
+S_LAST = 64
 S_STATS = {0: (3,)}
 LATE = ()
+M_PASS = 0
+COPY_AT = 1
+COPY_LATE = False
+PE_FIRST = False
+M_COLS = 216
 G_T = 0
 X0_ORDER = (0, 3, 1, 2)
 SPLIT = True
@@ -234,15 +239,33 @@ def tile_groupedlinear_t_kernel(tc, x, ln_gamma, ln_beta, W, b, out):
 
         gq_t = {}
 
-        def regroup(u, c2, eng, n0, n1):
+        def gq_tile(u):
             if u not in gq_t:
                 gq_t[u] = gqpool.tile([P, PASSES, UNIT, 4], BF16, tag="gq", name="gq%d" % u, align_bytes=64)
+
+        def regroup(u, c2, eng, n0, n1):
+            gq_tile(u)
             dst = gq_t[u][:, c2, n0:n1, :].rearrange("p (c i) t -> p c t i", i=4)
             src = pl_t[u][:, c2 * 4:(c2 + 1) * 4, n0:n1].rearrange("p t (c i) -> p c t i", i=4)
             if eng == "v":
                 nc.vector.tensor_copy(out=dst, in_=src)
             else:
                 nc.scalar.copy(out=dst, in_=src)
+
+        pm_t = {}
+
+        def interleave(u):
+            pm_t[u] = pst.tile([P, M_COLS, 4], BF16, tag="zt", name="pm%d" % u)
+            for n in range(0, M_COLS, M_COLS // 2):
+                n0 = UNIT - M_COLS + n
+                nc.tensor.matmul(out=pm_t[u][:, n:n + M_COLS // 2, :],
+                                 lhsT=ident_b[:],
+                                 rhs=pl_t[u][:, 4 * M_PASS:4 * M_PASS + 4, n0:n0 + M_COLS // 2].rearrange("p t n -> p n t"),
+                                 start=True, stop=True)
+
+        def interleaved(u):
+            nc.scalar.copy(out=gq_t[u][:, M_PASS, UNIT - M_COLS:UNIT, :].rearrange("p n t -> p (n t)"),
+                           in_=pm_t[u][:].rearrange("p n t -> p (n t)"))
 
         def quantise(u, c2, n0=0, n1=UNIT):
             if u not in xc_t:
@@ -377,8 +400,10 @@ def tile_groupedlinear_t_kernel(tc, x, ln_gamma, ln_beta, W, b, out):
                 load_w(i // UPG + 1)
             if live(i - 2) and i not in LATE:
                 store(i - 2)
+            if COPY_LATE and 0 <= i - 1 < UNITS - 1:
+                interleaved(i - 1)
             if live(i - 1):
-                regroup(i - 1, 0, "v", 0, UNIT)
+                regroup(i - 1, 0, "v", 0, UNIT if i - 1 == UNITS - 1 else UNIT - M_COLS)
                 if i - 1 < UNITS - 1:
                     regroup(i - 1, 1, "v", 0, UNIT - s_cols(i - 1))
                 quantise(i - 1, 0)
@@ -422,6 +447,11 @@ def tile_groupedlinear_t_kernel(tc, x, ln_gamma, ln_beta, W, b, out):
                 zrows(i + 1, "gv")
             if live(i):
                 banks(first, CHUNKS)
+            if i < UNITS - 1:
+                gq_tile(i)
+                interleave(i)
+                if COPY_AT == 0:
+                    interleaved(i)
             if i in LATE and i not in DEFER:
                 store(i - 2)
             if i == 0:
@@ -429,12 +459,17 @@ def tile_groupedlinear_t_kernel(tc, x, ln_gamma, ln_beta, W, b, out):
                 w_transpose(0, 1)
             if live(i + 1):
                 zrows(i + 1, "s")
+            if i < UNITS - 1 and COPY_AT == 1:
+                interleaved(i)
             if live(i):
-                regroup(i, 1, "s", UNIT - s_cols(i), UNIT)
-            if i in w_when:
-                w_transpose(*w_when[i])
+                if i == UNITS - 1:
+                    regroup(i, 1, "s", UNIT - s_cols(i), UNIT)
+                elif S_COLS:
+                    regroup(i, 1, "s", UNIT - s_cols(i), UNIT)
             if live(i - 1) and i + 1 not in DEFER and i - 1 < UNITS - 1:
                 multiply(i - 1)
+            if i in w_when:
+                w_transpose(*w_when[i])
             if live(i + 2):
                 for j in range(ROWT):
                     for h in range(2):

from contextlib import ExitStack

import concourse.mybir as mybir
from concourse.masks import make_identity

F32 = mybir.dt.float32
BF16 = mybir.dt.bfloat16
U32 = mybir.dt.uint32
U8 = mybir.dt.uint8
FP8X4 = mybir.dt.float8_e4m3fn_x4
ALU = mybir.AluOpType
ACT = mybir.ActivationFunctionType

P = 128
G = 4
K = 1024
O = 256
POS = 2048
UNIT = 512
UPG = POS // UNIT
UNITS = G * UPG
ROWT = UNIT // P
CHUNKS = K // P
PASSES = K // 512
OT = O // P
HALF = UNIT // 2
EPS = 1e-6
XBUFS = 6

FLOPS = 2 * G * POS * K * O

Z_ENGINE = ("g", "g", "g", "s")
Z_LAST = ("v", "v", "v", "v")
N_LAST = 1
S_COLS = 0
S_LAST = 64
S_STATS = {0: (3,)}
LATE = ()
M_PASS = 0
COPY_AT = 1
COPY_LATE = False
PE_FIRST = False
M_COLS = 216
G_T = 0
X0_ORDER = (0, 3, 1, 2)
SPLIT = True
DEFER = ()
FIRST = 1
FIRST1 = 3
V_BANKS = {}


def tile_groupedlinear_t_kernel(tc, x, ln_gamma, ln_beta, W, b, out):
    nc = tc.nc
    xv = x.rearrange("a (h b) c d -> (a h) (b c d)", h=2)
    ov = out.rearrange("o a b c -> o (a b c)")

    with ExitStack() as ctx:
        const = ctx.enter_context(tc.tile_pool(name="const", bufs=1))
        xpool = ctx.enter_context(tc.tile_pool(name="xpool", bufs=XBUFS))
        zpool = ctx.enter_context(tc.tile_pool(name="zpool", bufs=12))
        small = ctx.enter_context(tc.tile_pool(name="small", bufs=4))
        plpool = ctx.enter_context(tc.tile_pool(name="plpool", bufs=3))
        gqpool = ctx.enter_context(tc.tile_pool(name="gqpool", bufs=2))
        xcpool = ctx.enter_context(tc.tile_pool(name="xcpool", bufs=3))
        ypool = ctx.enter_context(tc.tile_pool(name="ypool", bufs=3))
        junkpool = ctx.enter_context(tc.tile_pool(name="junkpool", bufs=1))
        wstage = ctx.enter_context(tc.tile_pool(name="wstage", bufs=2))
        pst = ctx.enter_context(tc.psum_pool(name="pst", bufs=6))
        psy = ctx.enter_context(tc.psum_pool(name="psy", bufs=2))
        ctx.enter_context(tc.manual_schedule())

        x_t = {}
        mv_t = {}
        std_t = {}
        rstd_t = {}
        negmu_t = {}
        nmr_t = {}
        z_t = {}
        pl_t = {}
        xc_t = {}
        xsc_t = {}
        wg_t = {}

        def live(u):
            return 0 <= u < UNITS

        def load_x(u):
            xt = xpool.tile([P, ROWT, K], BF16, tag="x", name="xt%d" % u)
            rows = xv[u * UNIT:(u + 1) * UNIT, :].rearrange("(j p) k -> p j k", p=P)
            if u == 0:
                for j in X0_ORDER:
                    nc.sync.dma_start(out=xt[:, j, :], in_=rows[:, j, :])
            else:
                nc.sync.dma_start(out=xt[:], in_=rows)
            x_t[u] = xt

        w_raw = []
        for g in range(G):
            wr = const.tile([P, OT, K], BF16, name="wraw%d" % g)
            w_raw.append(wr)

        def load_w(g):
            nc.sync.dma_start(out=w_raw[g][:], in_=W[g].rearrange("(t o) k -> o t k", t=OT))

        load_x(0)
        prm = const.tile([P, 5, P], BF16, name="prm")
        nc.vector.memset(prm[:], 0.0)
        prmk = prm[:, 0:4, :].rearrange("p t q -> p (t q)")
        eps_t = const.tile([P, 1], F32, name="eps_t")
        nc.vector.memset(eps_t[:], EPS)
        nc.sync.dma_start(out=prmk[0:8, :], in_=ln_gamma.rearrange("g (c p) -> (g c) p", p=512))
        nc.sync.dma_start(out=prmk[8:16, :], in_=ln_beta.rearrange("g (c p) -> (g c) p", p=512))
        nc.sync.dma_start(out=prm[0:8, 4, :], in_=b.rearrange("g (c p) -> (g c) p", p=P))
        load_x(1)
        load_w(0)
        for u in range(2, XBUFS - 1):
            load_x(u)

        warm = const.tile([P, 1], F32, name="warm")
        nc.scalar.activation(out=warm[:], in_=eps_t[:], func=ACT.Sqrt)

        ident_b = const.tile([P, P], BF16, name="ident_b")
        make_identity(nc, ident_b[:])
        ident_f = const.tile([P, P], F32, name="ident_f")
        make_identity(nc, ident_f[:])

        cols = const.tile([P, 5, 16], F32, name="cols")

        def parameters():
            prm_ps = pst.tile([P, 5, P], BF16, tag="zt", name="prm_ps")
            for t in range(4):
                nc.tensor.transpose(prm_ps[:, t, :], prmk[:, t:512:4], ident_b[:])
            nc.tensor.transpose(prm_ps[:, 4, :], prm[:, 4, :], ident_b[:])
            nc.scalar.copy(out=cols[:], in_=prm_ps[:, :, 0:16])

        wc = const.tile([P, G, PASSES, O], U32, name="wc", align_bytes=64)
        ws = const.tile([P, G, PASSES, O], U8, name="ws", align_bytes=64)

        def w_transpose(g, c2):
            wt = pst.tile([P, OT, 2, P], F32, tag="zt", name="wt%d_%d" % (g, c2))
            for a in range(OT):
                words = w_raw[g][:, a, :].bitcast(F32)
                for e in range(2):
                    nc.tensor.transpose(wt[:, a, e, :], words[:, c2 * 256 + e:(c2 + 1) * 256:2], ident_f[:])
            wg = wstage.tile([P, OT, P, 4], BF16, tag="wg", name="wg%d_%d" % (g, c2), align_bytes=64)
            nc.scalar.copy(out=wg[:].rearrange("p a o t -> p (a o t)").bitcast(F32).rearrange("p (a o e) -> p a o e", a=OT, e=2),
                           in_=wt[:].rearrange("p a e o -> p a o e"))
            wg_t[(g, c2)] = wg

        def w_quantise(g, c2):
            nc.vector.quantize_mx(
                out=wc[:, g, c2, :].bitcast(FP8X4),
                scales=ws[:, g, c2, :],
                in_=wg_t[(g, c2)][:].rearrange("p a o t -> p (a o t)"),
            )

        w_when = {}
        for g in range(1, G):
            w_when[UPG * g - 2] = (g, 0)
            w_when[UPG * g - 1] = (g, 1)


        st_t = {}

        def stat_tiles(u):
            if u not in st_t:
                st_t[u] = small.tile([P, ROWT, 2, 6], F32, tag="st", name="st%d" % u)
                mv_t[u] = small.tile([P, ROWT, 2], F32, tag="mv", name="mv%d" % u)
                std_t[u] = small.tile([P, ROWT], F32, tag="std", name="std%d" % u)
                negmu_t[u] = small.tile([P, ROWT], F32, tag="negmu", name="negmu%d" % u)
                rstd_t[u] = small.tile([P, ROWT], F32, tag="rstd", name="rstd%d" % u)
                nmr_t[u] = small.tile([P, ROWT], F32, tag="nmr", name="nmr%d" % u)

        def v_rows(u):
            return [j for j in range(ROWT) if j not in S_STATS.get(u, ())]

        def bn(u, j, h):
            stat_tiles(u)
            nc.vector.bn_stats(out=st_t[u][:, j, h, :], in_=x_t[u][:, j, h * 512:(h + 1) * 512])

        def aggr(u, j):
            nc.vector.bn_aggr(out=mv_t[u][:, j, :], in_=st_t[u][:, j, :, :].rearrange("p h s -> p (h s)"))

        acc_t = {}

        def scalar_sum(u, j):
            stat_tiles(u)
            junk = junkpool.tile([P, K], BF16, tag="junk", name="junka%d_%d" % (u, j))
            acc_t[(u, j)] = small.tile([P, 2], F32, tag="acc", name="acc%d_%d" % (u, j))
            nc.scalar.activation(out=junk[:], in_=x_t[u][:, j, :], func=ACT.Identity, accum_out=acc_t[(u, j)][:, 0:1])
            nc.scalar.activation(out=negmu_t[u][:, j:j + 1], in_=acc_t[(u, j)][:, 0:1], func=ACT.Copy, scale=-1.0 / K)

        def scalar_square(u, j):
            junk = junkpool.tile([P, K], BF16, tag="junk", name="junkb%d_%d" % (u, j))
            nc.scalar.activation(out=junk[:], in_=x_t[u][:, j, :], func=ACT.Square, scale=1.0,
                                 bias=negmu_t[u][:, j:j + 1], accum_out=acc_t[(u, j)][:, 1:2])
            nc.scalar.activation(out=std_t[u][:, j:j + 1], in_=acc_t[(u, j)][:, 1:2], func=ACT.Sqrt, bias=eps_t[:], scale=1.0 / K)

        def sqrt_negmean(u, j0, j1):
            nc.scalar.activation(out=std_t[u][:, j0:j1], in_=mv_t[u][:, j0:j1, 1], func=ACT.Sqrt, bias=eps_t[:], scale=1.0)
            nc.scalar.activation(out=negmu_t[u][:, j0:j1], in_=mv_t[u][:, j0:j1, 0], func=ACT.Copy, scale=-1.0)

        def recip(u, j0=0, j1=ROWT):
            nc.vector.reciprocal(out=rstd_t[u][:, j0:j1], in_=std_t[u][:, j0:j1])

        def negmean_rstd(u, j):
            nc.scalar.activation(out=nmr_t[u][:, j:j + 1], in_=negmu_t[u][:, j:j + 1], func=ACT.Copy,
                                 scale=rstd_t[u][:, j:j + 1])

        def zrow(u, j, eng, t0=0, t1=4):
            if (u, j) not in z_t:
                z_t[(u, j)] = zpool.tile([P, 4, K // 4], F32, tag="z", name="z%d_%d" % (u, j))
            z = z_t[(u, j)][:, t0:t1, :]
            xin = x_t[u][:, j, :].rearrange("p (q t) -> p t q", t=4)[:, t0:t1, :]
            if eng == "g":
                nc.gpsimd.tensor_scalar(out=z, in0=xin, scalar1=negmu_t[u][:, j:j + 1],
                                        scalar2=rstd_t[u][:, j:j + 1], op0=ALU.add, op1=ALU.mult)
            elif eng == "v":
                nc.vector.tensor_scalar(out=z, in0=xin, scalar1=negmu_t[u][:, j:j + 1],
                                        scalar2=rstd_t[u][:, j:j + 1], op0=ALU.add, op1=ALU.mult)
            else:
                nc.scalar.activation(out=z, in_=xin, func=ACT.Identity,
                                     scale=rstd_t[u][:, j:j + 1], bias=nmr_t[u][:, j:j + 1])

        def bank(u, c):
            g = u // UPG
            zp = pst.tile([P, UNIT], F32, tag="zt", name="zp%d_%d" % (u, c))
            c2, t = divmod(c, 4)
            for j in range(ROWT):
                nc.tensor.transpose(zp[:, j * P:(j + 1) * P], z_t[(u, j)][:, t, c2 * P:(c2 + 1) * P], ident_f[:])
            gi = g * PASSES + c2
            if c in V_BANKS.get(u, ()):
                nc.vector.tensor_scalar(out=pl_t[u][:, c, :], in0=zp[:], scalar1=cols[:, t, gi:gi + 1],
                                        scalar2=cols[:, t, 8 + gi:9 + gi], op0=ALU.mult, op1=ALU.add)
            else:
                nc.scalar.activation(out=pl_t[u][:, c, :], in_=zp[:], func=ACT.Identity,
                                     scale=cols[:, t, gi:gi + 1], bias=cols[:, t, 8 + gi:9 + gi])

        gq_t = {}

        def gq_tile(u):
            if u not in gq_t:
                gq_t[u] = gqpool.tile([P, PASSES, UNIT, 4], BF16, tag="gq", name="gq%d" % u, align_bytes=64)

        def regroup(u, c2, eng, n0, n1):
            gq_tile(u)
            dst = gq_t[u][:, c2, n0:n1, :].rearrange("p (c i) t -> p c t i", i=4)
            src = pl_t[u][:, c2 * 4:(c2 + 1) * 4, n0:n1].rearrange("p t (c i) -> p c t i", i=4)
            if eng == "v":
                nc.vector.tensor_copy(out=dst, in_=src)
            else:
                nc.scalar.copy(out=dst, in_=src)

        pm_t = {}

        def interleave(u):
            pm_t[u] = pst.tile([P, M_COLS, 4], BF16, tag="zt", name="pm%d" % u)
            for n in range(0, M_COLS, M_COLS // 2):
                n0 = UNIT - M_COLS + n
                nc.tensor.matmul(out=pm_t[u][:, n:n + M_COLS // 2, :],
                                 lhsT=ident_b[:],
                                 rhs=pl_t[u][:, 4 * M_PASS:4 * M_PASS + 4, n0:n0 + M_COLS // 2].rearrange("p t n -> p n t"),
                                 start=True, stop=True)

        def interleaved(u):
            nc.scalar.copy(out=gq_t[u][:, M_PASS, UNIT - M_COLS:UNIT, :].rearrange("p n t -> p (n t)"),
                           in_=pm_t[u][:].rearrange("p n t -> p (n t)"))

        def quantise(u, c2, n0=0, n1=UNIT):
            if u not in xc_t:
                xc_t[u] = xcpool.tile([P, PASSES, UNIT], U32, tag="xc", name="xc%d" % u, align_bytes=64)
                xsc_t[u] = xcpool.tile([P, PASSES, UNIT], U8, tag="xsc", name="xsc%d" % u, align_bytes=64)
            nc.vector.quantize_mx(
                out=xc_t[u][:, c2, n0:n1].bitcast(FP8X4),
                scales=xsc_t[u][:, c2, n0:n1],
                in_=gq_t[u][:, c2, n0:n1, :].rearrange("p n t -> p (n t)"),
            )

        yps_t = {}

        def multiply(u):
            g = u // UPG
            yps = []
            for a in range(OT):
                yp = psy.tile([P, UNIT], F32, tag="yp", name="yp%d_%d" % (u, a))
                yps.append(yp)
            for c2 in range(PASSES):
                for a in range(OT):
                    nc.tensor.matmul_mx(
                        out=yps[a][:],
                        lhsT=wc[:, g, c2, a * P:(a + 1) * P].bitcast(FP8X4),
                        lhsT_scale=ws[:, g, c2, a * P:(a + 1) * P],
                        rhs=xc_t[u][:, c2, :].bitcast(FP8X4),
                        rhs_scale=xsc_t[u][:, c2, :],
                        start=(c2 == 0),
                        stop=(c2 == PASSES - 1),
                    )
            yps_t[u] = yps

        last_t = {}

        def last_product(h, c2):
            u = UNITS - 1
            g = G - 1
            for a in range(OT):
                if c2 == 0:
                    last_t[(a, h)] = pst.tile([P, HALF], F32, tag="zt", name="ylast%d_%d" % (a, h))
                nc.tensor.matmul_mx(
                    out=last_t[(a, h)][:],
                    lhsT=wc[:, g, c2, a * P:(a + 1) * P].bitcast(FP8X4),
                    lhsT_scale=ws[:, g, c2, a * P:(a + 1) * P],
                    rhs=xc_t[u][:, c2, h * HALF:(h + 1) * HALF].bitcast(FP8X4),
                    rhs_scale=xsc_t[u][:, c2, h * HALF:(h + 1) * HALF],
                    start=(c2 == 0),
                    stop=(c2 == PASSES - 1),
                )

        def last_store(h, engines):
            g = G - 1
            if h == 0:
                last_t["y"] = ypool.tile([P, OT, UNIT], F32, tag="y", name="ylast")
            for a in range(OT):
                bi = g * OT + a
                src = last_t[(a, h)][:]
                dst = last_t["y"][:, a, h * HALF:(h + 1) * HALF]
                if engines[a] == "v":
                    nc.vector.tensor_scalar(out=dst, in0=src, scalar1=cols[:, 4, bi:bi + 1], scalar2=None, op0=ALU.add)
                else:
                    nc.scalar.activation(out=dst, in_=src, func=ACT.Identity, bias=cols[:, 4, bi:bi + 1], scale=1.0)
                p0 = (UPG - 1) * UNIT + h * HALF
                nc.sync.dma_start(out=ov[bi * P:(bi + 1) * P, p0:p0 + HALF], in_=dst)

        def store(u):
            g = u // UPG
            q = u % UPG
            yps = yps_t[u]
            ysb = ypool.tile([P, OT, UNIT], F32, tag="y", name="y%d" % u)
            dst = ov[g * O:(g + 1) * O, q * UNIT:(q + 1) * UNIT].rearrange("(t o) n -> o t n", t=OT)
            for a in range(OT):
                bi = g * OT + a
                nc.scalar.activation(out=ysb[:, a, :], in_=yps[a][:], func=ACT.Identity,
                                     bias=cols[:, 4, bi:bi + 1], scale=1.0)
            nc.sync.dma_start(out=dst, in_=ysb[:])

        def z_engine(u):
            return Z_LAST if u >= UNITS - N_LAST else Z_ENGINE

        def s_cols(u):
            return S_LAST if u == UNITS - 1 else S_COLS

        def zrows(u, engines):
            for j in range(ROWT):
                if z_engine(u)[j] in engines:
                    if z_engine(u)[j] == "s":
                        negmean_rstd(u, j)
                    zrow(u, j, z_engine(u)[j], G_T if z_engine(u)[j] == "s" else 0, 4)
            if "g" in engines and z_engine(u)[3] == "s" and G_T:
                zrow(u, 3, "g", 0, G_T)

        s0 = S_STATS.get(0, ())
        s1 = S_STATS.get(1, ())
        n0 = ROWT - len(s0)
        if s0:
            scalar_sum(0, 3)
        for j in range(n0):
            bn(0, j, 0)
            bn(0, j, 1)
            if j:
                recip(0, j - 1, j)
                zrow(0, j - 1, "g")
            aggr(0, j)
            sqrt_negmean(0, j, j + 1)
            if j == 0 and s0:
                scalar_square(0, 3)
        bn(1, 0, 0)
        recip(0, n0 - 1, 4)
        if s0:
            zrow(0, 2, "g")
        if s1:
            scalar_sum(1, 3)
        negmean_rstd(0, 3)
        zrow(0, 3, "s")
        bn(1, 0, 1)
        if s1:
            scalar_square(1, 3)
        for j in range(1, ROWT):
            if j not in s1:
                bn(1, j, 0)
                bn(1, j, 1)
        for j in range(ROWT):
            if j not in s1:
                aggr(1, j)
        parameters()

        for i in range(UNITS + 1):
            if live(i + XBUFS - 1):
                load_x(i + XBUFS - 1)
            if i % UPG == 0 and i // UPG + 1 < G:
                load_w(i // UPG + 1)
            if live(i - 2) and i not in LATE:
                store(i - 2)
            if COPY_LATE and 0 <= i - 1 < UNITS - 1:
                interleaved(i - 1)
            if live(i - 1):
                regroup(i - 1, 0, "v", 0, UNIT if i - 1 == UNITS - 1 else UNIT - M_COLS)
                if i - 1 < UNITS - 1:
                    regroup(i - 1, 1, "v", 0, UNIT - s_cols(i - 1))
                quantise(i - 1, 0)
                if i - 1 in w_when:
                    w_quantise(*w_when[i - 1])
                if i == 1:
                    w_quantise(0, 0)
                    w_quantise(0, 1)
                if i - 1 == UNITS - 1:
                    last_product(0, 0)
                    last_product(1, 0)
                    regroup(i - 1, 1, "v", 0, HALF)
                    regroup(i - 1, 1, "v", HALF, UNIT - s_cols(i - 1))
                    quantise(i - 1, 1, 0, HALF)
                    last_product(0, 1)
                    quantise(i - 1, 1, HALF, UNIT)
                    last_product(1, 1)
                    last_store(0, "ss")
                    last_store(1, "sv")
            if i == 0:
                bn(i + 2, 0, 0)
                bn(i + 2, 0, 1)

            def banks(c0, c1):
                for c in range(c0, c1):
                    bank(i, c)

            first = FIRST if i else FIRST1
            if live(i):
                pl_t[i] = plpool.tile([P, CHUNKS, UNIT], BF16, tag="pl", name="pl%d" % i)
                banks(0, first)
            if live(i + 1):
                sqrt_negmean(i + 1, 0, ROWT - len(S_STATS.get(i + 1, ())))
                recip(i + 1)
            if i in DEFER:
                multiply(i - 2)
                store(i - 2)
            if live(i - 1) and i - 1 < UNITS - 1:
                quantise(i - 1, 1)
            if live(i + 1):
                zrows(i + 1, "gv")
            if live(i):
                banks(first, CHUNKS)
            if i < UNITS - 1:
                gq_tile(i)
                interleave(i)
                if COPY_AT == 0:
                    interleaved(i)
            if i in LATE and i not in DEFER:
                store(i - 2)
            if i == 0:
                w_transpose(0, 0)
                w_transpose(0, 1)
            if live(i + 1):
                zrows(i + 1, "s")
            if i < UNITS - 1 and COPY_AT == 1:
                interleaved(i)
            if live(i):
                if i == UNITS - 1:
                    regroup(i, 1, "s", UNIT - s_cols(i), UNIT)
                elif S_COLS:
                    regroup(i, 1, "s", UNIT - s_cols(i), UNIT)
            if live(i - 1) and i + 1 not in DEFER and i - 1 < UNITS - 1:
                multiply(i - 1)
            if i in w_when:
                w_transpose(*w_when[i])
            if live(i + 2):
                for j in range(ROWT):
                    for h in range(2):
                        if i or j:
                            bn(i + 2, j, h)
                for j in range(ROWT):
                    aggr(i + 2, j)
